import numpy as np
import ml_dtypes


def mxq(x, axis, fmt="e4m3"):
    dtype, down = {"e4m3": (ml_dtypes.float8_e4m3fn, 7), "e5m2": (ml_dtypes.float8_e5m2, 14)}[fmt]
    v = np.moveaxis(np.asarray(x, np.float32).astype(ml_dtypes.bfloat16).astype(np.float64), axis, -1)
    blocks = v.reshape(v.shape[:-1] + (-1, 32))
    amax = np.abs(blocks).max(-1, keepdims=True)
    byte = np.maximum(np.where(amax > 0, np.frexp(amax)[1] - 1 + 127, 0) - down, 1)
    scale = np.exp2(byte - 127.0)
    codes = (blocks / scale).astype(np.float32).astype(dtype).astype(np.float64)
    return np.moveaxis((codes * scale).reshape(v.shape), -1, axis)


WIDE = False


def mx_kscale(k):
    if not WIDE:
        return np.ones(k)
    levels = np.array([10, -10, 5, -5, 0])
    a = np.random.permutation(np.resize(levels, k // 512 * 4)).reshape(k // 512, 4)
    idx = np.arange(k)
    return np.exp2(a[idx // 512, idx % 128 // 32])


BF16 = ml_dtypes.bfloat16


def bf(x):
    return np.asarray(x, np.float32).astype(BF16)


def f64(x):
    return np.asarray(x).astype(np.float64)


B, DIM = 6144, 512


def setup_inputs():
    s = mx_kscale(DIM)
    p = np.random.standard_normal((B, DIM)) / s
    q = np.random.standard_normal((B, DIM)) * s
    A = np.random.standard_normal((DIM, DIM)) * 0.7 / np.sqrt(DIM) / s[:, None] / s[None, :]
    return {"pq": bf(np.concatenate([p, q], axis=1)), "A": bf(A)}


def reference(pq, A):
    pq, A = f64(pq), f64(A)
    S = A + A.T
    p = pq[..., :DIM]
    q = pq[..., DIM:]
    pterm = mxq(q, 1, "e4m3") @ mxq(S, 1, "e4m3").T
    return np.concatenate([p + pterm, q], axis=-1)

@@ -1,0 +1,149 @@
+from contextlib import ExitStack
+
+import concourse.mybir as mybir
+from concourse.masks import make_identity
+
+BF16 = mybir.dt.bfloat16
+F32 = mybir.dt.float32
+U32 = mybir.dt.uint32
+U8 = mybir.dt.uint8
+FP8X4 = mybir.dt.float8_e4m3fn_x4
+ADD = mybir.AluOpType.add
+
+P = 128
+B = 6144
+DIM = 512
+TILES = B // P
+GROUP = 4
+GROUPS = TILES // GROUP
+LOAD_TILES = (4, 4, 8, 8, 8, 8, 8)
+OUT_BUFS = 5
+
+FLOPS = 2 * B * DIM * DIM
+BYTES = B * 2 * DIM * 2 + DIM * DIM * 2 + B * 2 * DIM * 4
+
+
+def tile_linear_sub_t_kernel(tc, pq, A, out):
+    nc = tc.nc
+    with ExitStack() as ctx:
+        const = ctx.enter_context(tc.tile_pool(name="const", bufs=1))
+        resident = ctx.enter_context(tc.tile_pool(name="resident", bufs=1))
+        stage = ctx.enter_context(tc.tile_pool(name="stage", bufs=3))
+        results = ctx.enter_context(tc.tile_pool(name="results", bufs=OUT_BUFS))
+        psum_t = ctx.enter_context(tc.psum_pool(name="psum_t", bufs=4))
+        psum_o = ctx.enter_context(tc.psum_pool(name="psum_o", bufs=4))
+
+        pq_rows = pq.rearrange("(p t) c -> p t c", t=TILES)
+        out_rows = out.rearrange("(p t) c -> p t c", t=TILES)
+
+        a_rows = const.tile([P, 4 * DIM], BF16, name="a_rows")
+        nc.sync.dma_start(
+            out=a_rows[:].rearrange("p (u c e) -> p u c e", u=2, c=2),
+            in_=A.rearrange("(u p c) e -> p u c e", u=2, p=P, c=2),
+        )
+        where = []
+        first = 0
+        for n, width in enumerate(LOAD_TILES):
+            chunk = resident.tile([P, width * 2 * DIM], BF16, name="pq%d" % n)
+            nc.sync.dma_start(
+                out=chunk[:].rearrange("p (t c) -> p t c", c=2 * DIM),
+                in_=pq_rows[:, first : first + width, :],
+            )
+            for j in range(0, width, GROUP):
+                where.append((chunk, j))
+            first += width
+
+        ident = const.tile([P, P], F32, name="ident")
+        make_identity(nc, ident[:])
+
+        a_words = a_rows[:].bitcast(F32).rearrange("p (a b w) -> p a b w", a=2, b=2)
+        s_grouped = const.tile([P, 4 * DIM], BF16, name="s_grouped", align_bytes=64)
+        s_view = s_grouped[:].rearrange(
+            "p (a r b u c) -> p a u r b c", a=2, r=P, b=2, u=2, c=2
+        )
+        a_view = a_rows[:].rearrange("p (u c a r b) -> p u a r b c", u=2, c=2, a=2, r=P, b=2)
+        for u in range(2):
+            at = psum_t.tile([P, DIM], F32, name="xt")
+            at_out = at[:].rearrange("p (a b r) -> p a b r", a=2, b=2)
+            for a in range(2):
+                for b in range(2):
+                    nc.tensor.transpose(
+                        at_out[:, a, b, :], a_words[:, a, b, P * u : P * (u + 1)], ident[:]
+                    )
+            at_view = at[:].bitcast(BF16).rearrange(
+                "p (a b r c) -> p a r b c", a=2, b=2, r=P, c=2
+            )
+            for a in range(2):
+                nc.vector.tensor_tensor(
+                    out=s_view[:, a, u], in0=at_view[:, a], in1=a_view[:, u, a], op=ADD
+                )
+        s_codes = const.tile([P, DIM], U32, name="s_codes", align_bytes=64)
+        s_scales = const.tile([P, DIM], U8, name="s_scales", align_bytes=64)
+        nc.vector.quantize_mx(
+            out=s_codes[:].bitcast(FP8X4), scales=s_scales[:], in_=s_grouped[:]
+        )
+
+        grouped = {}
+        quantised = {}
+
+        def transpose_group(g):
+            chunk, j0 = where[g]
+            words = chunk[:].bitcast(F32).rearrange("p (t w) -> p t w", w=DIM)
+            q_grouped = stage.tile([P, GROUP * DIM], BF16, name="q_grouped", align_bytes=64)
+            q_pairs = q_grouped[:].bitcast(F32).rearrange(
+                "p (i r u) -> p i r u", i=GROUP, r=P, u=2
+            )
+            for h in range(GROUP // 2):
+                xt = psum_t.tile([P, DIM], F32, name="xt")
+                xt_out = xt[:].rearrange("p (i u r) -> p i u r", i=2, u=2)
+                for i in range(2):
+                    for u in range(2):
+                        lo = DIM // 2 + P * u
+                        nc.tensor.transpose(
+                            xt_out[:, i, u, :], words[:, j0 + 2 * h + i, lo : lo + P], ident[:]
+                        )
+                nc.scalar.copy(
+                    out=q_pairs[:, 2 * h : 2 * h + 2],
+                    in_=xt[:].rearrange("p (i u r) -> p i r u", i=2, u=2),
+                )
+            grouped[g] = q_grouped
+
+        def quantise_group(g):
+            q_codes = stage.tile([P, GROUP * P], U32, name="q_codes", align_bytes=64)
+            q_scales = stage.tile([P, GROUP * P], U8, name="q_scales", align_bytes=64)
+            nc.vector.quantize_mx(
+                out=q_codes[:].bitcast(FP8X4), scales=q_scales[:], in_=grouped[g][:]
+            )
+            quantised[g] = (q_codes, q_scales)
+
+        def multiply_group(g):
+            chunk, j0 = where[g]
+            rows = chunk[:].rearrange("p (t c) -> p t c", c=2 * DIM)
+            q_codes, q_scales = quantised[g]
+            res = results.tile([P, GROUP, 2 * DIM], F32, name="res")
+            for i in range(GROUP):
+                acc = psum_o.tile([P, DIM], F32, name="acc")
+                nc.tensor.matmul_mx(
+                    out=acc[:],
+                    lhsT=q_codes[:, P * i : P * (i + 1)].bitcast(FP8X4),
+                    lhsT_scale=q_scales[:, P * i : P * (i + 1)],
+                    rhs=s_codes[:].bitcast(FP8X4),
+                    rhs_scale=s_scales[:],
+                    start=True,
+                    stop=True,
+                )
+                nc.vector.tensor_tensor(
+                    out=res[:, i, 0:DIM], in0=acc[:], in1=rows[:, j0 + i, 0:DIM], op=ADD
+                )
+            nc.scalar.copy(out=res[:, :, DIM : 2 * DIM], in_=rows[:, j0 : j0 + GROUP, DIM : 2 * DIM])
+            nc.sync.dma_start(out=out_rows[:, GROUP * g : GROUP * (g + 1), :], in_=res[:])
+
+        transpose_group(0)
+        transpose_group(1)
+        quantise_group(0)
+        for g in range(GROUPS):
+            if g + 2 < GROUPS:
+                transpose_group(g + 2)
+            if g + 1 < GROUPS:
+                quantise_group(g + 1)
+            multiply_group(g)

@@ -16,8 +16,9 @@ DIM = 512
 TILES = B // P
 GROUP = 4
 GROUPS = TILES // GROUP
-LOAD_TILES = (4, 4, 8, 8, 8, 8, 8)
-OUT_BUFS = 5
+LOAD_TILES = (8, 8, 16, 16)
+STORE_GROUPS = 2
+OUT_BUFS = 3
 
 FLOPS = 2 * B * DIM * DIM
 BYTES = B * 2 * DIM * 2 + DIM * DIM * 2 + B * 2 * DIM * 4
@@ -85,6 +86,7 @@ def tile_linear_sub_t_kernel(tc, pq, A, out):
 
         grouped = {}
         quantised = {}
+        open_res = {}
 
         def transpose_group(g):
             chunk, j0 = where[g]
@@ -120,7 +122,12 @@ def tile_linear_sub_t_kernel(tc, pq, A, out):
             chunk, j0 = where[g]
             rows = chunk[:].rearrange("p (t c) -> p t c", c=2 * DIM)
             q_codes, q_scales = quantised[g]
-            res = results.tile([P, GROUP, 2 * DIM], F32, name="res")
+            part = g % STORE_GROUPS
+            if part == 0:
+                new_res = results.tile([P, STORE_GROUPS * GROUP, 2 * DIM], F32, name="res")
+                open_res[0] = new_res
+            whole = open_res[0]
+            res = whole[:, GROUP * part : GROUP * (part + 1), :]
             for i in range(GROUP):
                 acc = psum_o.tile([P, DIM], F32, name="acc")
                 nc.tensor.matmul_mx(
@@ -136,7 +143,11 @@ def tile_linear_sub_t_kernel(tc, pq, A, out):
                     out=res[:, i, 0:DIM], in0=acc[:], in1=rows[:, j0 + i, 0:DIM], op=ADD
                 )
             nc.scalar.copy(out=res[:, :, DIM : 2 * DIM], in_=rows[:, j0 : j0 + GROUP, DIM : 2 * DIM])
-            nc.sync.dma_start(out=out_rows[:, GROUP * g : GROUP * (g + 1), :], in_=res[:])
+            if part == STORE_GROUPS - 1:
+                last = GROUP * (g + 1)
+                nc.sync.dma_start(
+                    out=out_rows[:, last - STORE_GROUPS * GROUP : last, :], in_=whole[:]
+                )
 
         transpose_group(0)
         transpose_group(1)

@@ -39,8 +39,8 @@ def tile_linear_sub_t_kernel(tc, pq, A, out):
 
         a_rows = const.tile([P, 4 * DIM], BF16, name="a_rows")
         nc.sync.dma_start(
-            out=a_rows[:].rearrange("p (u c e) -> p u c e", u=2, c=2),
-            in_=A.rearrange("(u p c) e -> p u c e", u=2, p=P, c=2),
+            out=a_rows[:].rearrange("p (t e) -> p t e", t=4),
+            in_=A.rearrange("(p t) e -> p t e", t=4),
         )
         where = []
         first = 0
@@ -57,27 +57,17 @@ def tile_linear_sub_t_kernel(tc, pq, A, out):
         ident = const.tile([P, P], F32, name="ident")
         make_identity(nc, ident[:])
 
-        a_words = a_rows[:].bitcast(F32).rearrange("p (a b w) -> p a b w", a=2, b=2)
+        a_words = a_rows[:].bitcast(F32).rearrange("p (s w u) -> p s u w", s=4, w=P, u=2)
         s_grouped = const.tile([P, 4 * DIM], BF16, name="s_grouped", align_bytes=64)
-        s_view = s_grouped[:].rearrange(
-            "p (a r b u c) -> p a u r b c", a=2, r=P, b=2, u=2, c=2
-        )
-        a_view = a_rows[:].rearrange("p (u c a r b) -> p u a r b c", u=2, c=2, a=2, r=P, b=2)
+        s_view = s_grouped[:].rearrange("p (r s u c) -> p u r s c", r=P, s=4, u=2, c=2)
+        a_view = a_rows[:].rearrange("p (u c r s) -> p u r s c", u=2, c=2, r=P, s=4)
         for u in range(2):
             at = psum_t.tile([P, DIM], F32, name="xt")
-            at_out = at[:].rearrange("p (a b r) -> p a b r", a=2, b=2)
-            for a in range(2):
-                for b in range(2):
-                    nc.tensor.transpose(
-                        at_out[:, a, b, :], a_words[:, a, b, P * u : P * (u + 1)], ident[:]
-                    )
-            at_view = at[:].bitcast(BF16).rearrange(
-                "p (a b r c) -> p a r b c", a=2, b=2, r=P, c=2
-            )
-            for a in range(2):
-                nc.vector.tensor_tensor(
-                    out=s_view[:, a, u], in0=at_view[:, a], in1=a_view[:, u, a], op=ADD
-                )
+            at_out = at[:].rearrange("p (s r) -> p s r", s=4)
+            for s in range(4):
+                nc.tensor.transpose(at_out[:, s, :], a_words[:, s, u, :], ident[:])
+            at_view = at[:].bitcast(BF16).rearrange("p (s r c) -> p r s c", s=4, r=P, c=2)
+            nc.vector.tensor_tensor(out=s_view[:, u], in0=at_view, in1=a_view[:, u], op=ADD)
         s_codes = const.tile([P, DIM], U32, name="s_codes", align_bytes=64)
         s_scales = const.tile([P, DIM], U8, name="s_scales", align_bytes=64)
         nc.vector.quantize_mx(
@@ -90,7 +80,9 @@ def tile_linear_sub_t_kernel(tc, pq, A, out):
 
         def transpose_group(g):
             chunk, j0 = where[g]
-            words = chunk[:].bitcast(F32).rearrange("p (t w) -> p t w", w=DIM)
+            words = chunk[:].bitcast(F32).rearrange(
+                "p (t h w u) -> p t h u w", h=2, w=P, u=2
+            )
             q_grouped = stage.tile([P, GROUP * DIM], BF16, name="q_grouped", align_bytes=64)
             q_pairs = q_grouped[:].bitcast(F32).rearrange(
                 "p (i r u) -> p i r u", i=GROUP, r=P, u=2
@@ -100,9 +92,8 @@ def tile_linear_sub_t_kernel(tc, pq, A, out):
                 xt_out = xt[:].rearrange("p (i u r) -> p i u r", i=2, u=2)
                 for i in range(2):
                     for u in range(2):
-                        lo = DIM // 2 + P * u
                         nc.tensor.transpose(
-                            xt_out[:, i, u, :], words[:, j0 + 2 * h + i, lo : lo + P], ident[:]
+                            xt_out[:, i, u, :], words[:, j0 + 2 * h + i, 1, u, :], ident[:]
                         )
                 nc.scalar.copy(
                     out=q_pairs[:, 2 * h : 2 * h + 2],

@@ -38,7 +38,7 @@ def tile_linear_sub_t_kernel(tc, pq, A, out):
         out_rows = out.rearrange("(p t) c -> p t c", t=TILES)
 
         a_rows = const.tile([P, 4 * DIM], BF16, name="a_rows")
-        nc.sync.dma_start(
+        nc.scalar.dma_start(
             out=a_rows[:].rearrange("p (t e) -> p t e", t=4),
             in_=A.rearrange("(p t) e -> p t e", t=4),
         )
@@ -46,7 +46,7 @@ def tile_linear_sub_t_kernel(tc, pq, A, out):
         first = 0
         for n, width in enumerate(LOAD_TILES):
             chunk = resident.tile([P, width * 2 * DIM], BF16, name="pq%d" % n)
-            nc.sync.dma_start(
+            nc.scalar.dma_start(
                 out=chunk[:].rearrange("p (t c) -> p t c", c=2 * DIM),
                 in_=pq_rows[:, first : first + width, :],
             )

@@ -18,7 +18,9 @@ GROUP = 4
 GROUPS = TILES // GROUP
 LOAD_TILES = (8, 8, 16, 16)
 STORE_GROUPS = 2
-OUT_BUFS = 3
+KIB = 1024
+PQ_TILE_BYTES = 2 * DIM * 2
+RES_OFFSETS = (96 * KIB, 128 * KIB, 160 * KIB, 0, 32 * KIB, 96 * KIB)
 
 FLOPS = 2 * B * DIM * DIM
 BYTES = B * 2 * DIM * 2 + DIM * DIM * 2 + B * 2 * DIM * 4
@@ -28,9 +30,8 @@ def tile_linear_sub_t_kernel(tc, pq, A, out):
     nc = tc.nc
     with ExitStack() as ctx:
         const = ctx.enter_context(tc.tile_pool(name="const", bufs=1))
-        resident = ctx.enter_context(tc.tile_pool(name="resident", bufs=1))
+        large = ctx.enter_context(tc.tile_pool(name="large", bufs=1))
         stage = ctx.enter_context(tc.tile_pool(name="stage", bufs=3))
-        results = ctx.enter_context(tc.tile_pool(name="results", bufs=OUT_BUFS))
         psum_t = ctx.enter_context(tc.psum_pool(name="psum_t", bufs=4))
         psum_o = ctx.enter_context(tc.psum_pool(name="psum_o", bufs=4))
 
@@ -45,7 +46,9 @@ def tile_linear_sub_t_kernel(tc, pq, A, out):
         where = []
         first = 0
         for n, width in enumerate(LOAD_TILES):
-            chunk = resident.tile([P, width * 2 * DIM], BF16, name="pq%d" % n)
+            chunk = large.tile(
+                [P, width * 2 * DIM], BF16, name="pq%d" % n, offset=first * PQ_TILE_BYTES
+            )
             nc.scalar.dma_start(
                 out=chunk[:].rearrange("p (t c) -> p t c", c=2 * DIM),
                 in_=pq_rows[:, first : first + width, :],
@@ -115,7 +118,12 @@ def tile_linear_sub_t_kernel(tc, pq, A, out):
             q_codes, q_scales = quantised[g]
             part = g % STORE_GROUPS
             if part == 0:
-                new_res = results.tile([P, STORE_GROUPS * GROUP, 2 * DIM], F32, name="res")
+                new_res = large.tile(
+                    [P, STORE_GROUPS * GROUP, 2 * DIM],
+                    F32,
+                    name="res%d" % (g // STORE_GROUPS),
+                    offset=RES_OFFSETS[g // STORE_GROUPS],
+                )
                 open_res[0] = new_res
             whole = open_res[0]
             res = whole[:, GROUP * part : GROUP * (part + 1), :]

@@ -19,6 +19,7 @@ GROUPS = TILES // GROUP
 LOAD_TILES = (8, 8, 16, 16)
 STORE_GROUPS = 2
 KIB = 1024
+LARGE_ALIGN = 4 * KIB
 PQ_TILE_BYTES = 2 * DIM * 2
 RES_OFFSETS = (96 * KIB, 128 * KIB, 160 * KIB, 0, 32 * KIB, 96 * KIB)
 
@@ -47,7 +48,11 @@ def tile_linear_sub_t_kernel(tc, pq, A, out):
         first = 0
         for n, width in enumerate(LOAD_TILES):
             chunk = large.tile(
-                [P, width * 2 * DIM], BF16, name="pq%d" % n, offset=first * PQ_TILE_BYTES
+                [P, width * 2 * DIM],
+                BF16,
+                name="pq%d" % n,
+                offset=first * PQ_TILE_BYTES,
+                align_bytes=LARGE_ALIGN,
             )
             nc.scalar.dma_start(
                 out=chunk[:].rearrange("p (t c) -> p t c", c=2 * DIM),
@@ -123,6 +128,7 @@ def tile_linear_sub_t_kernel(tc, pq, A, out):
                     F32,
                     name="res%d" % (g // STORE_GROUPS),
                     offset=RES_OFFSETS[g // STORE_GROUPS],
+                    align_bytes=LARGE_ALIGN,
                 )
                 open_res[0] = new_res
             whole = open_res[0]

@@ -16,12 +16,13 @@ DIM = 512
 TILES = B // P
 GROUP = 4
 GROUPS = TILES // GROUP
-LOAD_TILES = (8, 8, 16, 16)
-STORE_GROUPS = 2
+LOAD_TILES = (8, 8, 32)
+STORE_TILES = (8, 16, 16, 8)
 KIB = 1024
 LARGE_ALIGN = 4 * KIB
 PQ_TILE_BYTES = 2 * DIM * 2
-RES_OFFSETS = (96 * KIB, 128 * KIB, 160 * KIB, 0, 32 * KIB, 96 * KIB)
+PQ_OFFSET = 96 * KIB
+RES_OFFSETS = (64 * KIB, 0, 64 * KIB, 0)
 
 FLOPS = 2 * B * DIM * DIM
 BYTES = B * 2 * DIM * 2 + DIM * DIM * 2 + B * 2 * DIM * 4
@@ -51,7 +52,7 @@ def tile_linear_sub_t_kernel(tc, pq, A, out):
                 [P, width * 2 * DIM],
                 BF16,
                 name="pq%d" % n,
-                offset=first * PQ_TILE_BYTES,
+                offset=PQ_OFFSET + first * PQ_TILE_BYTES,
                 align_bytes=LARGE_ALIGN,
             )
             nc.scalar.dma_start(
@@ -61,6 +62,12 @@ def tile_linear_sub_t_kernel(tc, pq, A, out):
             for j in range(0, width, GROUP):
                 where.append((chunk, j))
             first += width
+
+        store_of = []
+        for n, width in enumerate(STORE_TILES):
+            begin = len(store_of)
+            for j in range(width // GROUP):
+                store_of.append((n, begin, width))
 
         ident = const.tile([P, P], F32, name="ident")
         make_identity(nc, ident[:])
@@ -121,13 +128,14 @@ def tile_linear_sub_t_kernel(tc, pq, A, out):
             chunk, j0 = where[g]
             rows = chunk[:].rearrange("p (t c) -> p t c", c=2 * DIM)
             q_codes, q_scales = quantised[g]
-            part = g % STORE_GROUPS
+            store, begin, width = store_of[g]
+            part = g - begin
             if part == 0:
                 new_res = large.tile(
-                    [P, STORE_GROUPS * GROUP, 2 * DIM],
+                    [P, width, 2 * DIM],
                     F32,
-                    name="res%d" % (g // STORE_GROUPS),
-                    offset=RES_OFFSETS[g // STORE_GROUPS],
+                    name="res%d" % store,
+                    offset=RES_OFFSETS[store],
                     align_bytes=LARGE_ALIGN,
                 )
                 open_res[0] = new_res
@@ -148,11 +156,9 @@ def tile_linear_sub_t_kernel(tc, pq, A, out):
                     out=res[:, i, 0:DIM], in0=acc[:], in1=rows[:, j0 + i, 0:DIM], op=ADD
                 )
             nc.scalar.copy(out=res[:, :, DIM : 2 * DIM], in_=rows[:, j0 : j0 + GROUP, DIM : 2 * DIM])
-            if part == STORE_GROUPS - 1:
+            if GROUP * (part + 1) == width:
                 last = GROUP * (g + 1)
-                nc.sync.dma_start(
-                    out=out_rows[:, last - STORE_GROUPS * GROUP : last, :], in_=whole[:]
-                )
+                nc.sync.dma_start(out=out_rows[:, last - width : last, :], in_=whole[:])
 
         transpose_group(0)
         transpose_group(1)

@@ -16,13 +16,13 @@ DIM = 512
 TILES = B // P
 GROUP = 4
 GROUPS = TILES // GROUP
-LOAD_TILES = (8, 8, 32)
-STORE_TILES = (8, 16, 16, 8)
+LOAD_TILES = (8, 16, 24)
+STORE_TILES = (12, 12, 12, 12)
 KIB = 1024
 LARGE_ALIGN = 4 * KIB
 PQ_TILE_BYTES = 2 * DIM * 2
-PQ_OFFSET = 96 * KIB
-RES_OFFSETS = (64 * KIB, 0, 64 * KIB, 0)
+PQ_OFFSET = 0
+RES_OFFSETS = (96 * KIB, 144 * KIB, 0, 96 * KIB)
 
 FLOPS = 2 * B * DIM * DIM
 BYTES = B * 2 * DIM * 2 + DIM * DIM * 2 + B * 2 * DIM * 4

@@ -164,8 +164,18 @@ def tile_linear_sub_t_kernel(tc, pq, A, out):
         transpose_group(1)
         quantise_group(0)
         for g in range(GROUPS):
-            if g + 2 < GROUPS:
-                transpose_group(g + 2)
-            if g + 1 < GROUPS:
-                quantise_group(g + 1)
+            next_two = [t for t in (g + 2,) if t < GROUPS]
+            next_one = [t for t in (g + 1,) if t < GROUPS]
+            early_two = [t for t in next_two if where[t][0] is where[g][0]]
+            early_one = [t for t in next_one if where[t][0] is where[g][0]]
+            for t in early_two:
+                transpose_group(t)
+            for t in early_one:
+                quantise_group(t)
             multiply_group(g)
+            for t in next_two:
+                if t not in early_two:
+                    transpose_group(t)
+            for t in next_one:
+                if t not in early_one:
+                    quantise_group(t)

@@ -160,6 +160,7 @@ def tile_linear_sub_t_kernel(tc, pq, A, out):
                 last = GROUP * (g + 1)
                 nc.sync.dma_start(out=out_rows[:, last - width : last, :], in_=whole[:])
 
+        ctx.enter_context(tc.manual_schedule())
         transpose_group(0)
         transpose_group(1)
         quantise_group(0)

@@ -16,13 +16,15 @@ DIM = 512
 TILES = B // P
 GROUP = 4
 GROUPS = TILES // GROUP
-LOAD_TILES = (8, 16, 24)
+LOAD_TILES = (16, 32)
 STORE_TILES = (12, 12, 12, 12)
 KIB = 1024
 LARGE_ALIGN = 4 * KIB
 PQ_TILE_BYTES = 2 * DIM * 2
-PQ_OFFSET = 0
-RES_OFFSETS = (96 * KIB, 144 * KIB, 0, 96 * KIB)
+PQ_OFFSET = 112 * KIB
+RES_OFFSETS = (0, 48 * KIB, 96 * KIB, 0)
+A_OFFSET = 0
+S_OFFSET = 4 * KIB
 
 FLOPS = 2 * B * DIM * DIM
 BYTES = B * 2 * DIM * 2 + DIM * DIM * 2 + B * 2 * DIM * 4
@@ -40,7 +42,9 @@ def tile_linear_sub_t_kernel(tc, pq, A, out):
         pq_rows = pq.rearrange("(p t) c -> p t c", t=TILES)
         out_rows = out.rearrange("(p t) c -> p t c", t=TILES)
 
-        a_rows = const.tile([P, 4 * DIM], BF16, name="a_rows")
+        a_rows = large.tile(
+            [P, 4 * DIM], BF16, name="a_rows", offset=A_OFFSET, align_bytes=LARGE_ALIGN
+        )
         nc.scalar.dma_start(
             out=a_rows[:].rearrange("p (t e) -> p t e", t=4),
             in_=A.rearrange("(p t) e -> p t e", t=4),
@@ -73,7 +77,9 @@ def tile_linear_sub_t_kernel(tc, pq, A, out):
         make_identity(nc, ident[:])
 
         a_words = a_rows[:].bitcast(F32).rearrange("p (s w u) -> p s u w", s=4, w=P, u=2)
-        s_grouped = const.tile([P, 4 * DIM], BF16, name="s_grouped", align_bytes=64)
+        s_grouped = large.tile(
+            [P, 4 * DIM], BF16, name="s_grouped", offset=S_OFFSET, align_bytes=LARGE_ALIGN
+        )
         s_view = s_grouped[:].rearrange("p (r s u c) -> p u r s c", r=P, s=4, u=2, c=2)
         a_view = a_rows[:].rearrange("p (u c r s) -> p u r s c", u=2, c=2, r=P, s=4)
         for u in range(2):
@@ -161,22 +167,16 @@ def tile_linear_sub_t_kernel(tc, pq, A, out):
                 nc.sync.dma_start(out=out_rows[:, last - width : last, :], in_=whole[:])
 
         ctx.enter_context(tc.manual_schedule())
-        transpose_group(0)
-        transpose_group(1)
-        quantise_group(0)
-        for g in range(GROUPS):
-            next_two = [t for t in (g + 2,) if t < GROUPS]
-            next_one = [t for t in (g + 1,) if t < GROUPS]
-            early_two = [t for t in next_two if where[t][0] is where[g][0]]
-            early_one = [t for t in next_one if where[t][0] is where[g][0]]
-            for t in early_two:
-                transpose_group(t)
-            for t in early_one:
-                quantise_group(t)
-            multiply_group(g)
-            for t in next_two:
-                if t not in early_two:
-                    transpose_group(t)
-            for t in next_one:
-                if t not in early_one:
-                    quantise_group(t)
+        begin = 0
+        for width in LOAD_TILES:
+            end = begin + width // GROUP
+            transpose_group(begin)
+            transpose_group(begin + 1)
+            quantise_group(begin)
+            for g in range(begin, end):
+                if g + 2 < end:
+                    transpose_group(g + 2)
+                if g + 1 < end:
+                    quantise_group(g + 1)
+                multiply_group(g)
+            begin = end

@@ -59,7 +59,7 @@ def tile_linear_sub_t_kernel(tc, pq, A, out):
                 offset=PQ_OFFSET + first * PQ_TILE_BYTES,
                 align_bytes=LARGE_ALIGN,
             )
-            nc.scalar.dma_start(
+            nc.sync.dma_start(
                 out=chunk[:].rearrange("p (t c) -> p t c", c=2 * DIM),
                 in_=pq_rows[:, first : first + width, :],
             )

from contextlib import ExitStack

import concourse.mybir as mybir
from concourse.masks import make_identity

BF16 = mybir.dt.bfloat16
F32 = mybir.dt.float32
U32 = mybir.dt.uint32
U8 = mybir.dt.uint8
FP8X4 = mybir.dt.float8_e4m3fn_x4
ADD = mybir.AluOpType.add

P = 128
B = 6144
DIM = 512
TILES = B // P
GROUP = 4
GROUPS = TILES // GROUP
LOAD_TILES = (16, 32)
STORE_TILES = (12, 12, 12, 12)
KIB = 1024
LARGE_ALIGN = 4 * KIB
PQ_TILE_BYTES = 2 * DIM * 2
PQ_OFFSET = 112 * KIB
RES_OFFSETS = (0, 48 * KIB, 96 * KIB, 0)
A_OFFSET = 0
S_OFFSET = 4 * KIB

FLOPS = 2 * B * DIM * DIM
BYTES = B * 2 * DIM * 2 + DIM * DIM * 2 + B * 2 * DIM * 4


def tile_linear_sub_t_kernel(tc, pq, A, out):
    nc = tc.nc
    with ExitStack() as ctx:
        const = ctx.enter_context(tc.tile_pool(name="const", bufs=1))
        large = ctx.enter_context(tc.tile_pool(name="large", bufs=1))
        stage = ctx.enter_context(tc.tile_pool(name="stage", bufs=3))
        psum_t = ctx.enter_context(tc.psum_pool(name="psum_t", bufs=4))
        psum_o = ctx.enter_context(tc.psum_pool(name="psum_o", bufs=4))

        pq_rows = pq.rearrange("(p t) c -> p t c", t=TILES)
        out_rows = out.rearrange("(p t) c -> p t c", t=TILES)

        a_rows = large.tile(
            [P, 4 * DIM], BF16, name="a_rows", offset=A_OFFSET, align_bytes=LARGE_ALIGN
        )
        nc.scalar.dma_start(
            out=a_rows[:].rearrange("p (t e) -> p t e", t=4),
            in_=A.rearrange("(p t) e -> p t e", t=4),
        )
        where = []
        first = 0
        for n, width in enumerate(LOAD_TILES):
            chunk = large.tile(
                [P, width * 2 * DIM],
                BF16,
                name="pq%d" % n,
                offset=PQ_OFFSET + first * PQ_TILE_BYTES,
                align_bytes=LARGE_ALIGN,
            )
            nc.sync.dma_start(
                out=chunk[:].rearrange("p (t c) -> p t c", c=2 * DIM),
                in_=pq_rows[:, first : first + width, :],
            )
            for j in range(0, width, GROUP):
                where.append((chunk, j))
            first += width

        store_of = []
        for n, width in enumerate(STORE_TILES):
            begin = len(store_of)
            for j in range(width // GROUP):
                store_of.append((n, begin, width))

        ident = const.tile([P, P], F32, name="ident")
        make_identity(nc, ident[:])

        a_words = a_rows[:].bitcast(F32).rearrange("p (s w u) -> p s u w", s=4, w=P, u=2)
        s_grouped = large.tile(
            [P, 4 * DIM], BF16, name="s_grouped", offset=S_OFFSET, align_bytes=LARGE_ALIGN
        )
        s_view = s_grouped[:].rearrange("p (r s u c) -> p u r s c", r=P, s=4, u=2, c=2)
        a_view = a_rows[:].rearrange("p (u c r s) -> p u r s c", u=2, c=2, r=P, s=4)
        for u in range(2):
            at = psum_t.tile([P, DIM], F32, name="xt")
            at_out = at[:].rearrange("p (s r) -> p s r", s=4)
            for s in range(4):
                nc.tensor.transpose(at_out[:, s, :], a_words[:, s, u, :], ident[:])
            at_view = at[:].bitcast(BF16).rearrange("p (s r c) -> p r s c", s=4, r=P, c=2)
            nc.vector.tensor_tensor(out=s_view[:, u], in0=at_view, in1=a_view[:, u], op=ADD)
        s_codes = const.tile([P, DIM], U32, name="s_codes", align_bytes=64)
        s_scales = const.tile([P, DIM], U8, name="s_scales", align_bytes=64)
        nc.vector.quantize_mx(
            out=s_codes[:].bitcast(FP8X4), scales=s_scales[:], in_=s_grouped[:]
        )

        grouped = {}
        quantised = {}
        open_res = {}

        def transpose_group(g):
            chunk, j0 = where[g]
            words = chunk[:].bitcast(F32).rearrange(
                "p (t h w u) -> p t h u w", h=2, w=P, u=2
            )
            q_grouped = stage.tile([P, GROUP * DIM], BF16, name="q_grouped", align_bytes=64)
            q_pairs = q_grouped[:].bitcast(F32).rearrange(
                "p (i r u) -> p i r u", i=GROUP, r=P, u=2
            )
            for h in range(GROUP // 2):
                xt = psum_t.tile([P, DIM], F32, name="xt")
                xt_out = xt[:].rearrange("p (i u r) -> p i u r", i=2, u=2)
                for i in range(2):
                    for u in range(2):
                        nc.tensor.transpose(
                            xt_out[:, i, u, :], words[:, j0 + 2 * h + i, 1, u, :], ident[:]
                        )
                nc.scalar.copy(
                    out=q_pairs[:, 2 * h : 2 * h + 2],
                    in_=xt[:].rearrange("p (i u r) -> p i r u", i=2, u=2),
                )
            grouped[g] = q_grouped

        def quantise_group(g):
            q_codes = stage.tile([P, GROUP * P], U32, name="q_codes", align_bytes=64)
            q_scales = stage.tile([P, GROUP * P], U8, name="q_scales", align_bytes=64)
            nc.vector.quantize_mx(
                out=q_codes[:].bitcast(FP8X4), scales=q_scales[:], in_=grouped[g][:]
            )
            quantised[g] = (q_codes, q_scales)

        def multiply_group(g):
            chunk, j0 = where[g]
            rows = chunk[:].rearrange("p (t c) -> p t c", c=2 * DIM)
            q_codes, q_scales = quantised[g]
            store, begin, width = store_of[g]
            part = g - begin
            if part == 0:
                new_res = large.tile(
                    [P, width, 2 * DIM],
                    F32,
                    name="res%d" % store,
                    offset=RES_OFFSETS[store],
                    align_bytes=LARGE_ALIGN,
                )
                open_res[0] = new_res
            whole = open_res[0]
            res = whole[:, GROUP * part : GROUP * (part + 1), :]
            for i in range(GROUP):
                acc = psum_o.tile([P, DIM], F32, name="acc")
                nc.tensor.matmul_mx(
                    out=acc[:],
                    lhsT=q_codes[:, P * i : P * (i + 1)].bitcast(FP8X4),
                    lhsT_scale=q_scales[:, P * i : P * (i + 1)],
                    rhs=s_codes[:].bitcast(FP8X4),
                    rhs_scale=s_scales[:],
                    start=True,
                    stop=True,
                )
                nc.vector.tensor_tensor(
                    out=res[:, i, 0:DIM], in0=acc[:], in1=rows[:, j0 + i, 0:DIM], op=ADD
                )
            nc.scalar.copy(out=res[:, :, DIM : 2 * DIM], in_=rows[:, j0 : j0 + GROUP, DIM : 2 * DIM])
            if GROUP * (part + 1) == width:
                last = GROUP * (g + 1)
                nc.sync.dma_start(out=out_rows[:, last - width : last, :], in_=whole[:])

        ctx.enter_context(tc.manual_schedule())
        begin = 0
        for width in LOAD_TILES:
            end = begin + width // GROUP
            transpose_group(begin)
            transpose_group(begin + 1)
            quantise_group(begin)
            for g in range(begin, end):
                if g + 2 < end:
                    transpose_group(g + 2)
                if g + 1 < end:
                    quantise_group(g + 1)
                multiply_group(g)
            begin = end
